import numpy as np
import ml_dtypes


def mxq(x, axis, fmt="e4m3"):
    dtype, down = {"e4m3": (ml_dtypes.float8_e4m3fn, 7), "e5m2": (ml_dtypes.float8_e5m2, 14)}[fmt]
    v = np.moveaxis(np.asarray(x, np.float32).astype(ml_dtypes.bfloat16).astype(np.float64), axis, -1)
    blocks = v.reshape(v.shape[:-1] + (-1, 32))
    amax = np.abs(blocks).max(-1, keepdims=True)
    byte = np.maximum(np.where(amax > 0, np.frexp(amax)[1] - 1 + 127, 0) - down, 1)
    scale = np.exp2(byte - 127.0)
    codes = (blocks / scale).astype(np.float32).astype(dtype).astype(np.float64)
    return np.moveaxis((codes * scale).reshape(v.shape), -1, axis)


WIDE = False


def mx_kscale(k):
    if not WIDE:
        return np.ones(k)
    levels = np.array([10, -10, 5, -5, 0])
    a = np.random.permutation(np.resize(levels, k // 512 * 4)).reshape(k // 512, 4)
    idx = np.arange(k)
    return np.exp2(a[idx // 512, idx % 128 // 32])


BF16 = ml_dtypes.bfloat16


def bf(x):
    return np.asarray(x, np.float32).astype(BF16)


def f64(x):
    return np.asarray(x).astype(np.float64)


N, C = 768, 512
KS = 3 * C
KV = 2 * C
G = KS + KV
SQRT3 = np.sqrt(3.0)


def silu(z):
    return z / (1.0 + np.exp(-z))


def setup_inputs():
    k = mx_kscale(KS)
    a = np.exp2(np.round(np.log2(k[C:KV]) / 2))
    b = np.exp2(np.round(np.log2(k[KV:]) / 2))
    f = np.concatenate([a, a * a, b * b])
    return {"s": bf(np.random.standard_normal((N, C)) * a),
            "v": bf(np.random.standard_normal((N, C, 3)) * b[:, None]),
            "w1": bf(np.random.standard_normal((KS, KS)) / f[:, None]),
            "w2": bf(np.random.standard_normal((KS, G)))}


def reference(s, v, w1, w2):
    s, v = f64(s), f64(v)
    ss = s * s
    vv0 = np.sum(v * v, axis=-1) / SQRT3
    sc = np.concatenate([s, ss, vv0], axis=-1)
    h = silu((mxq(sc, 1, "e4m3") @ mxq(f64(w1), 0, "e4m3")) / np.sqrt(KS))
    return (mxq(h, 1, "e4m3") @ mxq(f64(w2), 0, "e4m3")) / np.sqrt(KS)

@@ -1,0 +1,187 @@
+import math
+from contextlib import ExitStack
+
+import concourse.mybir as mybir
+from concourse.masks import make_identity
+
+BF16 = mybir.dt.bfloat16
+F32 = mybir.dt.float32
+U32 = mybir.dt.uint32
+U8 = mybir.dt.uint8
+FP8X4 = mybir.dt.float8_e4m3fn_x4
+ACT = mybir.ActivationFunctionType
+ALU = mybir.AluOpType
+
+P = 128
+PACK = 4
+K_PASS = P * PACK
+TOKENS = 768
+TILES = TOKENS // P
+C = 512
+KS = 3 * C
+PASSES = KS // K_PASS
+G = 5 * C
+CHUNK = 512
+W1_CHUNKS = KS // CHUNK
+W2_CHUNKS = G // CHUNK
+RAW_BUFS = 12
+W1_PIECES_PER_V_TILE = 2
+
+FLOPS = 2 * TOKENS * KS * (KS + G)
+
+
+def load_weight_piece(nc, raw_pool, w, chunk, g):
+    by_pass = w.rearrange("(g t p) n -> g p t n", t=PACK, p=P)
+    raw = raw_pool.tile([P, PACK, CHUNK], BF16, name="raw")
+    nc.sync.dma_start(out=raw[:], in_=by_pass[g, :, :, chunk * CHUNK : (chunk + 1) * CHUNK])
+    return raw
+
+
+def quantise_weight_chunk(nc, grouped_pool, pieces, codes, scales):
+    grouped = grouped_pool.tile([P, PASSES, CHUNK, PACK], BF16, name="grouped", align_bytes=64)
+    for g in range(PASSES):
+        nc.vector.tensor_copy(
+            out=grouped[:, g, :, :].rearrange("p (c i) t -> p c t i", i=4),
+            in_=pieces[g][:].rearrange("p t (c i) -> p c t i", i=4),
+        )
+    for g in range(PASSES):
+        nc.vector.quantize_mx(
+            out=codes[:, g, :].bitcast(FP8X4),
+            scales=scales[:, g, :],
+            in_=grouped[:, g, :, :].rearrange("p c t -> p (c t)"),
+        )
+
+
+def tile_selfinteraction_pa_kernel(tc, s, v, w1, w2, out):
+    nc = tc.nc
+    inv_sqrt_ks = 1.0 / math.sqrt(KS)
+
+    with ExitStack() as ctx:
+        keep = ctx.enter_context(tc.tile_pool(name="keep", bufs=1))
+        raw_pool = ctx.enter_context(tc.tile_pool(name="raw_pool", bufs=RAW_BUFS))
+        grouped_pool = ctx.enter_context(tc.tile_pool(name="grouped_pool", bufs=2))
+        work = ctx.enter_context(tc.tile_pool(name="work", bufs=2))
+        small = ctx.enter_context(tc.tile_pool(name="small", bufs=4))
+        store_pool = ctx.enter_context(tc.tile_pool(name="store_pool", bufs=6))
+        psum = ctx.enter_context(tc.psum_pool(name="psum", bufs=8))
+
+        s_sb = keep.tile([P, TILES, C], BF16, name="s_sb")
+        nc.sync.dma_start(out=s_sb[:], in_=s.rearrange("(p i) c -> p i c", i=TILES))
+        v_by_tile = v.rearrange("(p i) c d -> p i (c d)", i=TILES)
+        w1_order = [(m, g) for m in range(W1_CHUNKS) for g in range(PASSES)]
+        v_sb = []
+        w1_raw = {}
+        for i in range(TILES):
+            v_i = keep.tile([P, 3 * C], BF16, name="v_%d" % i)
+            nc.sync.dma_start(out=v_i[:], in_=v_by_tile[:, i, :])
+            v_sb.append(v_i)
+            for m, g in w1_order[W1_PIECES_PER_V_TILE * i : W1_PIECES_PER_V_TILE * (i + 1)]:
+                w1_raw[(m, g)] = load_weight_piece(nc, raw_pool, w1, m, g)
+        w2_raw = {}
+        for c in range(W2_CHUNKS):
+            for g in range(PASSES):
+                w2_raw[(c, g)] = load_weight_piece(nc, raw_pool, w2, c, g)
+
+        ident = keep.tile([P, P], BF16, name="ident")
+        make_identity(nc, ident[:])
+
+        warm = keep.tile([P, 1], F32, name="warm")
+        nc.vector.memset(warm[:], 0.0)
+        nc.scalar.activation(out=warm[:], in_=warm[:], func=ACT.Silu)
+
+        sc_codes = keep.tile([P, PASSES, TOKENS], U32, name="sc_codes", align_bytes=64)
+        sc_scales = keep.tile([P, PASSES, TOKENS], U8, name="sc_scales", align_bytes=64)
+        for i in range(TILES):
+            tokens = slice(i * P, (i + 1) * P)
+            squares = work.tile([P, C, 3], F32, name="squares")
+            nc.scalar.activation(
+                out=squares[:].rearrange("p c d -> p (c d)"),
+                in_=v_sb[i][:],
+                func=ACT.Square,
+                scale=3.0**-0.25,
+            )
+            computed = work.tile([P, 2, C], BF16, name="computed")
+            nc.vector.tensor_tensor(
+                out=computed[:, 0, :], in0=s_sb[:, i, :], in1=s_sb[:, i, :], op=ALU.mult
+            )
+            two = work.tile([P, C], F32, name="two")
+            nc.vector.tensor_tensor(
+                out=two[:], in0=squares[:, :, 0], in1=squares[:, :, 1], op=ALU.add
+            )
+            nc.vector.tensor_tensor(
+                out=computed[:, 1, :], in0=two[:], in1=squares[:, :, 2], op=ALU.add
+            )
+            sections = [s_sb[:, i, :], computed[:, 0, :], computed[:, 1, :]]
+            for g in range(PASSES):
+                flipped = psum.tile([P, PACK, P], BF16, name="flipped", tag="bank")
+                for t in range(PACK):
+                    nc.tensor.transpose(
+                        flipped[:, t, :], sections[g][:, t * P : (t + 1) * P], ident[:]
+                    )
+                sc_grouped = small.tile([P, P, PACK], BF16, name="sc_grouped", align_bytes=64)
+                nc.scalar.copy(out=sc_grouped[:], in_=flipped[:].rearrange("p t n -> p n t"))
+                nc.vector.quantize_mx(
+                    out=sc_codes[:, g, tokens].bitcast(FP8X4),
+                    scales=sc_scales[:, g, tokens],
+                    in_=sc_grouped[:].rearrange("p n t -> p (n t)"),
+                )
+
+        h_codes = keep.tile([P, PASSES, TOKENS], U32, name="h_codes", align_bytes=64)
+        h_scales = keep.tile([P, PASSES, TOKENS], U8, name="h_scales", align_bytes=64)
+        for m in range(W1_CHUNKS):
+            w1_codes = keep.tile([P, PASSES, CHUNK], U32, name="w1_codes_%d" % m, align_bytes=64)
+            w1_scales = keep.tile([P, PASSES, CHUNK], U8, name="w1_scales_%d" % m, align_bytes=64)
+            pieces = [w1_raw[(m, g)] for g in range(PASSES)]
+            quantise_weight_chunk(nc, grouped_pool, pieces, w1_codes, w1_scales)
+            for i in range(TILES):
+                tokens = slice(i * P, (i + 1) * P)
+                h_acc = psum.tile([P, PACK, P], F32, name="h_acc", tag="bank")
+                for t in range(PACK):
+                    columns = slice(t * P, (t + 1) * P)
+                    for g in range(PASSES):
+                        nc.tensor.matmul_mx(
+                            out=h_acc[:, t, :],
+                            lhsT=w1_codes[:, g, columns].bitcast(FP8X4),
+                            lhsT_scale=w1_scales[:, g, columns],
+                            rhs=sc_codes[:, g, tokens].bitcast(FP8X4),
+                            rhs_scale=sc_scales[:, g, tokens],
+                            start=(g == 0),
+                            stop=(g == PASSES - 1),
+                        )
+                h_grouped = small.tile([P, P, PACK], BF16, name="h_grouped", align_bytes=64)
+                nc.scalar.activation(
+                    out=h_grouped[:],
+                    in_=h_acc[:].rearrange("p t n -> p n t"),
+                    func=ACT.Silu,
+                    scale=inv_sqrt_ks,
+                )
+                nc.vector.quantize_mx(
+                    out=h_codes[:, m, tokens].bitcast(FP8X4),
+                    scales=h_scales[:, m, tokens],
+                    in_=h_grouped[:].rearrange("p n t -> p (n t)"),
+                )
+
+        out_by_tile = out.rearrange("(p i) n -> p i n", i=TILES)
+        for c in range(W2_CHUNKS):
+            w2_codes = keep.tile([P, PASSES, CHUNK], U32, name="w2_codes_%d" % c, align_bytes=64)
+            w2_scales = keep.tile([P, PASSES, CHUNK], U8, name="w2_scales_%d" % c, align_bytes=64)
+            pieces = [w2_raw[(c, g)] for g in range(PASSES)]
+            quantise_weight_chunk(nc, grouped_pool, pieces, w2_codes, w2_scales)
+            for i in range(TILES):
+                tokens = slice(i * P, (i + 1) * P)
+                out_acc = psum.tile([P, CHUNK], F32, name="out_acc", tag="bank")
+                for g in range(PASSES):
+                    nc.tensor.matmul_mx(
+                        out=out_acc[:],
+                        lhsT=h_codes[:, g, tokens].bitcast(FP8X4),
+                        lhsT_scale=h_scales[:, g, tokens],
+                        rhs=w2_codes[:, g, :].bitcast(FP8X4),
+                        rhs_scale=w2_scales[:, g, :],
+                        start=(g == 0),
+                        stop=(g == PASSES - 1),
+                    )
+                result = store_pool.tile([P, CHUNK], F32, name="result")
+                nc.scalar.mul(out=result[:], in_=out_acc[:], mul=inv_sqrt_ks)
+                nc.scalar.dma_start(
+                    out=out_by_tile[:, i, c * CHUNK : (c + 1) * CHUNK], in_=result[:]
+                )

@@ -26,6 +26,7 @@ W1_CHUNKS = KS // CHUNK
 W2_CHUNKS = G // CHUNK
 RAW_BUFS = 12
 W1_PIECES_PER_V_TILE = 2
+W2_SCALAR_COLUMNS = 64
 
 FLOPS = 2 * TOKENS * KS * (KS + G)
 
@@ -37,19 +38,25 @@ def load_weight_piece(nc, raw_pool, w, chunk, g):
     return raw
 
 
-def quantise_weight_chunk(nc, grouped_pool, pieces, codes, scales):
-    grouped = grouped_pool.tile([P, PASSES, CHUNK, PACK], BF16, name="grouped", align_bytes=64)
-    for g in range(PASSES):
-        nc.vector.tensor_copy(
-            out=grouped[:, g, :, :].rearrange("p (c i) t -> p c t i", i=4),
-            in_=pieces[g][:].rearrange("p t (c i) -> p c t i", i=4),
+def regroup_weight_piece(nc, grouped_pool, raw, scalar_columns):
+    grouped = grouped_pool.tile([P, CHUNK, PACK], BF16, name="grouped", align_bytes=64)
+    split = CHUNK - scalar_columns
+    nc.vector.tensor_copy(
+        out=grouped[:, :split, :].rearrange("p (c i) t -> p c t i", i=4),
+        in_=raw[:, :, :split].rearrange("p t (c i) -> p c t i", i=4),
+    )
+    if scalar_columns:
+        nc.scalar.copy(
+            out=grouped[:, split:, :].rearrange("p (c i) t -> p c t i", i=4),
+            in_=raw[:, :, split:].rearrange("p t (c i) -> p c t i", i=4),
         )
-    for g in range(PASSES):
-        nc.vector.quantize_mx(
-            out=codes[:, g, :].bitcast(FP8X4),
-            scales=scales[:, g, :],
-            in_=grouped[:, g, :, :].rearrange("p c t -> p (c t)"),
-        )
+    return grouped
+
+
+def quantise(nc, grouped, codes, scales):
+    nc.vector.quantize_mx(
+        out=codes.bitcast(FP8X4), scales=scales, in_=grouped.rearrange("p c t -> p (c t)")
+    )
 
 
 def tile_selfinteraction_pa_kernel(tc, s, v, w1, w2, out):
@@ -59,10 +66,10 @@ def tile_selfinteraction_pa_kernel(tc, s, v, w1, w2, out):
     with ExitStack() as ctx:
         keep = ctx.enter_context(tc.tile_pool(name="keep", bufs=1))
         raw_pool = ctx.enter_context(tc.tile_pool(name="raw_pool", bufs=RAW_BUFS))
-        grouped_pool = ctx.enter_context(tc.tile_pool(name="grouped_pool", bufs=2))
+        grouped_pool = ctx.enter_context(tc.tile_pool(name="grouped_pool", bufs=4))
         work = ctx.enter_context(tc.tile_pool(name="work", bufs=2))
         small = ctx.enter_context(tc.tile_pool(name="small", bufs=4))
-        store_pool = ctx.enter_context(tc.tile_pool(name="store_pool", bufs=6))
+        store_pool = ctx.enter_context(tc.tile_pool(name="store_pool", bufs=TILES))
         psum = ctx.enter_context(tc.psum_pool(name="psum", bufs=8))
 
         s_sb = keep.tile([P, TILES, C], BF16, name="s_sb")
@@ -89,10 +96,25 @@ def tile_selfinteraction_pa_kernel(tc, s, v, w1, w2, out):
         nc.vector.memset(warm[:], 0.0)
         nc.scalar.activation(out=warm[:], in_=warm[:], func=ACT.Silu)
 
-        sc_codes = keep.tile([P, PASSES, TOKENS], U32, name="sc_codes", align_bytes=64)
-        sc_scales = keep.tile([P, PASSES, TOKENS], U8, name="sc_scales", align_bytes=64)
+        sc_codes = keep.tile([P, TILES, PASSES, P], U32, name="sc_codes", align_bytes=64)
+        sc_scales = keep.tile([P, TILES, PASSES, P], U8, name="sc_scales", align_bytes=64)
         for i in range(TILES):
-            tokens = slice(i * P, (i + 1) * P)
+            s_flipped = psum.tile([P, PACK, P], BF16, name="s_flipped", tag="bank")
+            for t in range(PACK):
+                nc.tensor.transpose(s_flipped[:, t, :], s_sb[:, i, t * P : (t + 1) * P], ident[:])
+            s_grouped = small.tile([P, 2, P, PACK], BF16, name="s_grouped", align_bytes=64)
+            nc.scalar.copy(out=s_grouped[:, 0, :, :], in_=s_flipped[:].rearrange("p t n -> p n t"))
+            nc.scalar.activation(
+                out=s_grouped[:, 1, :, :],
+                in_=s_flipped[:].rearrange("p t n -> p n t"),
+                func=ACT.Square,
+            )
+            quantise(
+                nc,
+                s_grouped[:].rearrange("p g n t -> p (g n) t"),
+                sc_codes[:, i, 0:2, :].rearrange("p g n -> p (g n)"),
+                sc_scales[:, i, 0:2, :].rearrange("p g n -> p (g n)"),
+            )
             squares = work.tile([P, C, 3], F32, name="squares")
             nc.scalar.activation(
                 out=squares[:].rearrange("p c d -> p (c d)"),
@@ -100,39 +122,29 @@ def tile_selfinteraction_pa_kernel(tc, s, v, w1, w2, out):
                 func=ACT.Square,
                 scale=3.0**-0.25,
             )
-            computed = work.tile([P, 2, C], BF16, name="computed")
-            nc.vector.tensor_tensor(
-                out=computed[:, 0, :], in0=s_sb[:, i, :], in1=s_sb[:, i, :], op=ALU.mult
-            )
             two = work.tile([P, C], F32, name="two")
             nc.vector.tensor_tensor(
                 out=two[:], in0=squares[:, :, 0], in1=squares[:, :, 1], op=ALU.add
             )
-            nc.vector.tensor_tensor(
-                out=computed[:, 1, :], in0=two[:], in1=squares[:, :, 2], op=ALU.add
-            )
-            sections = [s_sb[:, i, :], computed[:, 0, :], computed[:, 1, :]]
-            for g in range(PASSES):
-                flipped = psum.tile([P, PACK, P], BF16, name="flipped", tag="bank")
-                for t in range(PACK):
-                    nc.tensor.transpose(
-                        flipped[:, t, :], sections[g][:, t * P : (t + 1) * P], ident[:]
-                    )
-                sc_grouped = small.tile([P, P, PACK], BF16, name="sc_grouped", align_bytes=64)
-                nc.scalar.copy(out=sc_grouped[:], in_=flipped[:].rearrange("p t n -> p n t"))
-                nc.vector.quantize_mx(
-                    out=sc_codes[:, g, tokens].bitcast(FP8X4),
-                    scales=sc_scales[:, g, tokens],
-                    in_=sc_grouped[:].rearrange("p n t -> p (n t)"),
-                )
+            vv0 = work.tile([P, C], BF16, name="vv0")
+            nc.vector.tensor_tensor(out=vv0[:], in0=two[:], in1=squares[:, :, 2], op=ALU.add)
+            v_flipped = psum.tile([P, PACK, P], BF16, name="v_flipped", tag="bank")
+            for t in range(PACK):
+                nc.tensor.transpose(v_flipped[:, t, :], vv0[:, t * P : (t + 1) * P], ident[:])
+            v_grouped = small.tile([P, P, PACK], BF16, name="v_grouped", align_bytes=64)
+            nc.scalar.copy(out=v_grouped[:], in_=v_flipped[:].rearrange("p t n -> p n t"))
+            quantise(nc, v_grouped[:], sc_codes[:, i, 2, :], sc_scales[:, i, 2, :])
 
         h_codes = keep.tile([P, PASSES, TOKENS], U32, name="h_codes", align_bytes=64)
         h_scales = keep.tile([P, PASSES, TOKENS], U8, name="h_scales", align_bytes=64)
         for m in range(W1_CHUNKS):
             w1_codes = keep.tile([P, PASSES, CHUNK], U32, name="w1_codes_%d" % m, align_bytes=64)
             w1_scales = keep.tile([P, PASSES, CHUNK], U8, name="w1_scales_%d" % m, align_bytes=64)
-            pieces = [w1_raw[(m, g)] for g in range(PASSES)]
-            quantise_weight_chunk(nc, grouped_pool, pieces, w1_codes, w1_scales)
+            grouped = [regroup_weight_piece(nc, grouped_pool, w1_raw[(m, 0)], 0)]
+            for g in range(PASSES):
+                if g + 1 < PASSES:
+                    grouped.append(regroup_weight_piece(nc, grouped_pool, w1_raw[(m, g + 1)], 0))
+                quantise(nc, grouped[g][:], w1_codes[:, g, :], w1_scales[:, g, :])
             for i in range(TILES):
                 tokens = slice(i * P, (i + 1) * P)
                 h_acc = psum.tile([P, PACK, P], F32, name="h_acc", tag="bank")
@@ -143,8 +155,8 @@ def tile_selfinteraction_pa_kernel(tc, s, v, w1, w2, out):
                             out=h_acc[:, t, :],
                             lhsT=w1_codes[:, g, columns].bitcast(FP8X4),
                             lhsT_scale=w1_scales[:, g, columns],
-                            rhs=sc_codes[:, g, tokens].bitcast(FP8X4),
-                            rhs_scale=sc_scales[:, g, tokens],
+                            rhs=sc_codes[:, i, g, :].bitcast(FP8X4),
+                            rhs_scale=sc_scales[:, i, g, :],
                             start=(g == 0),
                             stop=(g == PASSES - 1),
                         )
@@ -155,24 +167,28 @@ def tile_selfinteraction_pa_kernel(tc, s, v, w1, w2, out):
                     func=ACT.Silu,
                     scale=inv_sqrt_ks,
                 )
-                nc.vector.quantize_mx(
-                    out=h_codes[:, m, tokens].bitcast(FP8X4),
-                    scales=h_scales[:, m, tokens],
-                    in_=h_grouped[:].rearrange("p n t -> p (n t)"),
-                )
+                quantise(nc, h_grouped[:], h_codes[:, m, tokens], h_scales[:, m, tokens])
 
         out_by_tile = out.rearrange("(p i) n -> p i n", i=TILES)
         for c in range(W2_CHUNKS):
             w2_codes = keep.tile([P, PASSES, CHUNK], U32, name="w2_codes_%d" % c, align_bytes=64)
             w2_scales = keep.tile([P, PASSES, CHUNK], U8, name="w2_scales_%d" % c, align_bytes=64)
-            pieces = [w2_raw[(c, g)] for g in range(PASSES)]
-            quantise_weight_chunk(nc, grouped_pool, pieces, w2_codes, w2_scales)
-            for i in range(TILES):
-                tokens = slice(i * P, (i + 1) * P)
-                out_acc = psum.tile([P, CHUNK], F32, name="out_acc", tag="bank")
-                for g in range(PASSES):
+            out_acc = [
+                psum.tile([P, CHUNK], F32, name="out_acc_%d" % i, tag="bank") for i in range(TILES)
+            ]
+            grouped = [regroup_weight_piece(nc, grouped_pool, w2_raw[(c, 0)], W2_SCALAR_COLUMNS)]
+            for g in range(PASSES):
+                if g + 1 < PASSES:
+                    grouped.append(
+                        regroup_weight_piece(
+                            nc, grouped_pool, w2_raw[(c, g + 1)], W2_SCALAR_COLUMNS
+                        )
+                    )
+                quantise(nc, grouped[g][:], w2_codes[:, g, :], w2_scales[:, g, :])
+                for i in range(TILES):
+                    tokens = slice(i * P, (i + 1) * P)
                     nc.tensor.matmul_mx(
-                        out=out_acc[:],
+                        out=out_acc[i][:],
                         lhsT=h_codes[:, g, tokens].bitcast(FP8X4),
                         lhsT_scale=h_scales[:, g, tokens],
                         rhs=w2_codes[:, g, :].bitcast(FP8X4),
@@ -180,8 +196,9 @@ def tile_selfinteraction_pa_kernel(tc, s, v, w1, w2, out):
                         start=(g == 0),
                         stop=(g == PASSES - 1),
                     )
+            for i in range(TILES):
                 result = store_pool.tile([P, CHUNK], F32, name="result")
-                nc.scalar.mul(out=result[:], in_=out_acc[:], mul=inv_sqrt_ks)
-                nc.scalar.dma_start(
+                nc.scalar.mul(out=result[:], in_=out_acc[i][:], mul=inv_sqrt_ks)
+                nc.sync.dma_start(
                     out=out_by_tile[:, i, c * CHUNK : (c + 1) * CHUNK], in_=result[:]
                 )

@@ -10,7 +10,6 @@ U32 = mybir.dt.uint32
 U8 = mybir.dt.uint8
 FP8X4 = mybir.dt.float8_e4m3fn_x4
 ACT = mybir.ActivationFunctionType
-ALU = mybir.AluOpType
 
 P = 128
 PACK = 4
@@ -91,6 +90,8 @@ def tile_selfinteraction_pa_kernel(tc, s, v, w1, w2, out):
 
         ident = keep.tile([P, P], BF16, name="ident")
         make_identity(nc, ident[:])
+        ident_f32 = keep.tile([P, P], F32, name="ident_f32")
+        make_identity(nc, ident_f32[:])
 
         warm = keep.tile([P, 1], F32, name="warm")
         nc.vector.memset(warm[:], 0.0)
@@ -115,24 +116,26 @@ def tile_selfinteraction_pa_kernel(tc, s, v, w1, w2, out):
                 sc_codes[:, i, 0:2, :].rearrange("p g n -> p (g n)"),
                 sc_scales[:, i, 0:2, :].rearrange("p g n -> p (g n)"),
             )
-            squares = work.tile([P, C, 3], F32, name="squares")
+            squares = work.tile([P, 3, C], F32, name="squares")
             nc.scalar.activation(
-                out=squares[:].rearrange("p c d -> p (c d)"),
-                in_=v_sb[i][:],
+                out=squares[:],
+                in_=v_sb[i][:].rearrange("p (c d) -> p d c", d=3),
                 func=ACT.Square,
                 scale=3.0**-0.25,
             )
-            two = work.tile([P, C], F32, name="two")
-            nc.vector.tensor_tensor(
-                out=two[:], in0=squares[:, :, 0], in1=squares[:, :, 1], op=ALU.add
-            )
-            vv0 = work.tile([P, C], BF16, name="vv0")
-            nc.vector.tensor_tensor(out=vv0[:], in0=two[:], in1=squares[:, :, 2], op=ALU.add)
-            v_flipped = psum.tile([P, PACK, P], BF16, name="v_flipped", tag="bank")
+            vv0_flipped = psum.tile([P, PACK, P], F32, name="vv0_flipped", tag="bank")
             for t in range(PACK):
-                nc.tensor.transpose(v_flipped[:, t, :], vv0[:, t * P : (t + 1) * P], ident[:])
+                for d in range(3):
+                    nc.tensor.matmul(
+                        out=vv0_flipped[:, t, :],
+                        lhsT=squares[:, d, t * P : (t + 1) * P],
+                        rhs=ident_f32[:],
+                        is_transpose=True,
+                        start=(d == 0),
+                        stop=(d == 2),
+                    )
             v_grouped = small.tile([P, P, PACK], BF16, name="v_grouped", align_bytes=64)
-            nc.scalar.copy(out=v_grouped[:], in_=v_flipped[:].rearrange("p t n -> p n t"))
+            nc.vector.tensor_copy(out=v_grouped[:], in_=vv0_flipped[:].rearrange("p t n -> p n t"))
             quantise(nc, v_grouped[:], sc_codes[:, i, 2, :], sc_scales[:, i, 2, :])
 
         h_codes = keep.tile([P, PASSES, TOKENS], U32, name="h_codes", align_bytes=64)
@@ -198,7 +201,12 @@ def tile_selfinteraction_pa_kernel(tc, s, v, w1, w2, out):
                     )
             for i in range(TILES):
                 result = store_pool.tile([P, CHUNK], F32, name="result")
-                nc.scalar.mul(out=result[:], in_=out_acc[i][:], mul=inv_sqrt_ks)
+                if c == W2_CHUNKS - 1 and i % 2 == 1:
+                    nc.vector.tensor_scalar_mul(
+                        out=result[:], in0=out_acc[i][:], scalar1=inv_sqrt_ks
+                    )
+                else:
+                    nc.scalar.mul(out=result[:], in_=out_acc[i][:], mul=inv_sqrt_ks)
                 nc.sync.dma_start(
                     out=out_by_tile[:, i, c * CHUNK : (c + 1) * CHUNK], in_=result[:]
                 )

@@ -24,8 +24,6 @@ CHUNK = 512
 W1_CHUNKS = KS // CHUNK
 W2_CHUNKS = G // CHUNK
 RAW_BUFS = 12
-W1_PIECES_PER_V_TILE = 2
-W2_SCALAR_COLUMNS = 64
 
 FLOPS = 2 * TOKENS * KS * (KS + G)
 
@@ -37,18 +35,12 @@ def load_weight_piece(nc, raw_pool, w, chunk, g):
     return raw
 
 
-def regroup_weight_piece(nc, grouped_pool, raw, scalar_columns):
+def regroup_weight_piece(nc, grouped_pool, raw):
     grouped = grouped_pool.tile([P, CHUNK, PACK], BF16, name="grouped", align_bytes=64)
-    split = CHUNK - scalar_columns
     nc.vector.tensor_copy(
-        out=grouped[:, :split, :].rearrange("p (c i) t -> p c t i", i=4),
-        in_=raw[:, :, :split].rearrange("p t (c i) -> p c t i", i=4),
+        out=grouped[:].rearrange("p (c i) t -> p c t i", i=4),
+        in_=raw[:].rearrange("p t (c i) -> p c t i", i=4),
     )
-    if scalar_columns:
-        nc.scalar.copy(
-            out=grouped[:, split:, :].rearrange("p (c i) t -> p c t i", i=4),
-            in_=raw[:, :, split:].rearrange("p t (c i) -> p c t i", i=4),
-        )
     return grouped
 
 
@@ -74,14 +66,14 @@ def tile_selfinteraction_pa_kernel(tc, s, v, w1, w2, out):
         s_sb = keep.tile([P, TILES, C], BF16, name="s_sb")
         nc.sync.dma_start(out=s_sb[:], in_=s.rearrange("(p i) c -> p i c", i=TILES))
         v_by_tile = v.rearrange("(p i) c d -> p i (c d)", i=TILES)
-        w1_order = [(m, g) for m in range(W1_CHUNKS) for g in range(PASSES)]
         v_sb = []
-        w1_raw = {}
         for i in range(TILES):
             v_i = keep.tile([P, 3 * C], BF16, name="v_%d" % i)
             nc.sync.dma_start(out=v_i[:], in_=v_by_tile[:, i, :])
             v_sb.append(v_i)
-            for m, g in w1_order[W1_PIECES_PER_V_TILE * i : W1_PIECES_PER_V_TILE * (i + 1)]:
+        w1_raw = {}
+        for m in range(W1_CHUNKS):
+            for g in range(PASSES):
                 w1_raw[(m, g)] = load_weight_piece(nc, raw_pool, w1, m, g)
         w2_raw = {}
         for c in range(W2_CHUNKS):
@@ -143,10 +135,10 @@ def tile_selfinteraction_pa_kernel(tc, s, v, w1, w2, out):
         for m in range(W1_CHUNKS):
             w1_codes = keep.tile([P, PASSES, CHUNK], U32, name="w1_codes_%d" % m, align_bytes=64)
             w1_scales = keep.tile([P, PASSES, CHUNK], U8, name="w1_scales_%d" % m, align_bytes=64)
-            grouped = [regroup_weight_piece(nc, grouped_pool, w1_raw[(m, 0)], 0)]
+            grouped = [regroup_weight_piece(nc, grouped_pool, w1_raw[(m, 0)])]
             for g in range(PASSES):
                 if g + 1 < PASSES:
-                    grouped.append(regroup_weight_piece(nc, grouped_pool, w1_raw[(m, g + 1)], 0))
+                    grouped.append(regroup_weight_piece(nc, grouped_pool, w1_raw[(m, g + 1)]))
                 quantise(nc, grouped[g][:], w1_codes[:, g, :], w1_scales[:, g, :])
             for i in range(TILES):
                 tokens = slice(i * P, (i + 1) * P)
@@ -179,14 +171,10 @@ def tile_selfinteraction_pa_kernel(tc, s, v, w1, w2, out):
             out_acc = [
                 psum.tile([P, CHUNK], F32, name="out_acc_%d" % i, tag="bank") for i in range(TILES)
             ]
-            grouped = [regroup_weight_piece(nc, grouped_pool, w2_raw[(c, 0)], W2_SCALAR_COLUMNS)]
+            grouped = [regroup_weight_piece(nc, grouped_pool, w2_raw[(c, 0)])]
             for g in range(PASSES):
                 if g + 1 < PASSES:
-                    grouped.append(
-                        regroup_weight_piece(
-                            nc, grouped_pool, w2_raw[(c, g + 1)], W2_SCALAR_COLUMNS
-                        )
-                    )
+                    grouped.append(regroup_weight_piece(nc, grouped_pool, w2_raw[(c, g + 1)]))
                 quantise(nc, grouped[g][:], w2_codes[:, g, :], w2_scales[:, g, :])
                 for i in range(TILES):
                     tokens = slice(i * P, (i + 1) * P)

@@ -23,7 +23,8 @@ G = 5 * C
 CHUNK = 512
 W1_CHUNKS = KS // CHUNK
 W2_CHUNKS = G // CHUNK
-RAW_BUFS = 12
+RAW_BUFS = 14
+SCALAR_PIECES = (8, 11, 14)
 
 FLOPS = 2 * TOKENS * KS * (KS + G)
 
@@ -35,9 +36,10 @@ def load_weight_piece(nc, raw_pool, w, chunk, g):
     return raw
 
 
-def regroup_weight_piece(nc, grouped_pool, raw):
+def regroup_weight_piece(nc, grouped_pool, raw, on_scalar):
     grouped = grouped_pool.tile([P, CHUNK, PACK], BF16, name="grouped", align_bytes=64)
-    nc.vector.tensor_copy(
+    copy = nc.scalar.copy if on_scalar else nc.vector.tensor_copy
+    copy(
         out=grouped[:].rearrange("p (c i) t -> p c t i", i=4),
         in_=raw[:].rearrange("p t (c i) -> p c t i", i=4),
     )
@@ -58,27 +60,44 @@ def tile_selfinteraction_pa_kernel(tc, s, v, w1, w2, out):
         keep = ctx.enter_context(tc.tile_pool(name="keep", bufs=1))
         raw_pool = ctx.enter_context(tc.tile_pool(name="raw_pool", bufs=RAW_BUFS))
         grouped_pool = ctx.enter_context(tc.tile_pool(name="grouped_pool", bufs=4))
-        work = ctx.enter_context(tc.tile_pool(name="work", bufs=2))
+        work = ctx.enter_context(tc.tile_pool(name="work", bufs=3))
         small = ctx.enter_context(tc.tile_pool(name="small", bufs=4))
+        h_pool = ctx.enter_context(tc.tile_pool(name="h_pool", bufs=8))
         store_pool = ctx.enter_context(tc.tile_pool(name="store_pool", bufs=TILES))
         psum = ctx.enter_context(tc.psum_pool(name="psum", bufs=8))
 
-        s_sb = keep.tile([P, TILES, C], BF16, name="s_sb")
-        nc.sync.dma_start(out=s_sb[:], in_=s.rearrange("(p i) c -> p i c", i=TILES))
+        s_by_pair = s.rearrange("(p i) c -> p i c", i=TILES)
         v_by_tile = v.rearrange("(p i) c d -> p i (c d)", i=TILES)
+        s_sb = []
         v_sb = []
-        for i in range(TILES):
+        raw = {}
+
+        def load_s_pair(j):
+            s_j = keep.tile([P, 2, C], BF16, name="s_%d" % j)
+            nc.sync.dma_start(out=s_j[:], in_=s_by_pair[:, 2 * j : 2 * j + 2, :])
+            s_sb.append(s_j)
+
+        def load_v_tile(i):
             v_i = keep.tile([P, 3 * C], BF16, name="v_%d" % i)
             nc.sync.dma_start(out=v_i[:], in_=v_by_tile[:, i, :])
             v_sb.append(v_i)
-        w1_raw = {}
-        for m in range(W1_CHUNKS):
-            for g in range(PASSES):
-                w1_raw[(m, g)] = load_weight_piece(nc, raw_pool, w1, m, g)
-        w2_raw = {}
-        for c in range(W2_CHUNKS):
-            for g in range(PASSES):
-                w2_raw[(c, g)] = load_weight_piece(nc, raw_pool, w2, c, g)
+
+        pieces = [("w1", m, g) for m in range(W1_CHUNKS) for g in range(PASSES)]
+        pieces += [("w2", c, g) for c in range(W2_CHUNKS) for g in range(PASSES)]
+        weights = {"w1": w1, "w2": w2}
+
+        def load_piece(n):
+            name, chunk, g = pieces[n]
+            raw[(name, chunk, g)] = load_weight_piece(nc, raw_pool, weights[name], chunk, g)
+
+        load_s_pair(0)
+        for i in range(TILES):
+            load_piece(i)
+            load_v_tile(i)
+            if i < 2:
+                load_s_pair(i + 1)
+        for n in range(TILES, len(pieces)):
+            load_piece(n)
 
         ident = keep.tile([P, P], BF16, name="ident")
         make_identity(nc, ident[:])
@@ -91,23 +110,36 @@ def tile_selfinteraction_pa_kernel(tc, s, v, w1, w2, out):
 
         sc_codes = keep.tile([P, TILES, PASSES, P], U32, name="sc_codes", align_bytes=64)
         sc_scales = keep.tile([P, TILES, PASSES, P], U8, name="sc_scales", align_bytes=64)
-        for i in range(TILES):
-            s_flipped = psum.tile([P, PACK, P], BF16, name="s_flipped", tag="bank")
+
+        s_flipped = {}
+        s_grouped = {}
+        v_squares = {}
+        vv0_flipped = {}
+        v_grouped = {}
+
+        def flip_s(i):
+            s_i = s_sb[i // 2][:, i % 2, :]
+            flipped = psum.tile([P, PACK, P], BF16, name="s_flipped", tag="bank")
             for t in range(PACK):
-                nc.tensor.transpose(s_flipped[:, t, :], s_sb[:, i, t * P : (t + 1) * P], ident[:])
-            s_grouped = small.tile([P, 2, P, PACK], BF16, name="s_grouped", align_bytes=64)
-            nc.scalar.copy(out=s_grouped[:, 0, :, :], in_=s_flipped[:].rearrange("p t n -> p n t"))
-            nc.scalar.activation(
-                out=s_grouped[:, 1, :, :],
-                in_=s_flipped[:].rearrange("p t n -> p n t"),
-                func=ACT.Square,
-            )
+                nc.tensor.transpose(flipped[:, t, :], s_i[:, t * P : (t + 1) * P], ident[:])
+            s_flipped[i] = flipped
+
+        def group_s(i):
+            flipped = s_flipped[i][:].rearrange("p t n -> p n t")
+            both = small.tile([P, 2, P, PACK], BF16, name="s_grouped", align_bytes=64)
+            nc.scalar.copy(out=both[:, 0, :, :], in_=flipped)
+            nc.scalar.activation(out=both[:, 1, :, :], in_=flipped, func=ACT.Square)
+            s_grouped[i] = both
+
+        def quantise_s(i):
             quantise(
                 nc,
-                s_grouped[:].rearrange("p g n t -> p (g n) t"),
+                s_grouped[i][:].rearrange("p g n t -> p (g n) t"),
                 sc_codes[:, i, 0:2, :].rearrange("p g n -> p (g n)"),
                 sc_scales[:, i, 0:2, :].rearrange("p g n -> p (g n)"),
             )
+
+        def square_v(i):
             squares = work.tile([P, 3, C], F32, name="squares")
             nc.scalar.activation(
                 out=squares[:],
@@ -115,86 +147,191 @@ def tile_selfinteraction_pa_kernel(tc, s, v, w1, w2, out):
                 func=ACT.Square,
                 scale=3.0**-0.25,
             )
-            vv0_flipped = psum.tile([P, PACK, P], F32, name="vv0_flipped", tag="bank")
+            v_squares[i] = squares
+
+        def flip_v(i):
+            squares = v_squares[i]
+            flipped = psum.tile([P, PACK, P], F32, name="vv0_flipped", tag="bank")
             for t in range(PACK):
                 for d in range(3):
                     nc.tensor.matmul(
-                        out=vv0_flipped[:, t, :],
+                        out=flipped[:, t, :],
                         lhsT=squares[:, d, t * P : (t + 1) * P],
                         rhs=ident_f32[:],
                         is_transpose=True,
                         start=(d == 0),
                         stop=(d == 2),
                     )
-            v_grouped = small.tile([P, P, PACK], BF16, name="v_grouped", align_bytes=64)
-            nc.vector.tensor_copy(out=v_grouped[:], in_=vv0_flipped[:].rearrange("p t n -> p n t"))
-            quantise(nc, v_grouped[:], sc_codes[:, i, 2, :], sc_scales[:, i, 2, :])
+            vv0_flipped[i] = flipped
+
+        def group_v(i):
+            vv0 = small.tile([P, P, PACK], BF16, name="v_grouped", align_bytes=64)
+            nc.vector.tensor_copy(out=vv0[:], in_=vv0_flipped[i][:].rearrange("p t n -> p n t"))
+            v_grouped[i] = vv0
+
+        def quantise_v(i):
+            quantise(nc, v_grouped[i][:], sc_codes[:, i, 2, :], sc_scales[:, i, 2, :])
+
+        weight_codes = {}
+        weight_scales = {}
+        for name, chunks in (("w1", W1_CHUNKS), ("w2", W2_CHUNKS)):
+            for c in range(chunks):
+                weight_codes[(name, c)] = keep.tile(
+                    [P, PASSES, CHUNK], U32, name="%s_codes_%d" % (name, c), align_bytes=64
+                )
+                weight_scales[(name, c)] = keep.tile(
+                    [P, PASSES, CHUNK], U8, name="%s_scales_%d" % (name, c), align_bytes=64
+                )
+        grouped = {}
+
+        def regroup(n):
+            grouped[n] = regroup_weight_piece(
+                nc, grouped_pool, raw[pieces[n]], on_scalar=n in SCALAR_PIECES
+            )
+
+        def quantise_piece(n):
+            name, chunk, g = pieces[n]
+            quantise(
+                nc,
+                grouped[n][:],
+                weight_codes[(name, chunk)][:, g, :],
+                weight_scales[(name, chunk)][:, g, :],
+            )
 
         h_codes = keep.tile([P, PASSES, TOKENS], U32, name="h_codes", align_bytes=64)
         h_scales = keep.tile([P, PASSES, TOKENS], U8, name="h_scales", align_bytes=64)
-        for m in range(W1_CHUNKS):
-            w1_codes = keep.tile([P, PASSES, CHUNK], U32, name="w1_codes_%d" % m, align_bytes=64)
-            w1_scales = keep.tile([P, PASSES, CHUNK], U8, name="w1_scales_%d" % m, align_bytes=64)
-            grouped = [regroup_weight_piece(nc, grouped_pool, w1_raw[(m, 0)])]
-            for g in range(PASSES):
-                if g + 1 < PASSES:
-                    grouped.append(regroup_weight_piece(nc, grouped_pool, w1_raw[(m, g + 1)]))
-                quantise(nc, grouped[g][:], w1_codes[:, g, :], w1_scales[:, g, :])
-            for i in range(TILES):
-                tokens = slice(i * P, (i + 1) * P)
-                h_acc = psum.tile([P, PACK, P], F32, name="h_acc", tag="bank")
-                for t in range(PACK):
-                    columns = slice(t * P, (t + 1) * P)
-                    for g in range(PASSES):
-                        nc.tensor.matmul_mx(
-                            out=h_acc[:, t, :],
-                            lhsT=w1_codes[:, g, columns].bitcast(FP8X4),
-                            lhsT_scale=w1_scales[:, g, columns],
-                            rhs=sc_codes[:, i, g, :].bitcast(FP8X4),
-                            rhs_scale=sc_scales[:, i, g, :],
-                            start=(g == 0),
-                            stop=(g == PASSES - 1),
-                        )
-                h_grouped = small.tile([P, P, PACK], BF16, name="h_grouped", align_bytes=64)
-                nc.scalar.activation(
-                    out=h_grouped[:],
-                    in_=h_acc[:].rearrange("p t n -> p n t"),
-                    func=ACT.Silu,
-                    scale=inv_sqrt_ks,
-                )
-                quantise(nc, h_grouped[:], h_codes[:, m, tokens], h_scales[:, m, tokens])
 
-        out_by_tile = out.rearrange("(p i) n -> p i n", i=TILES)
-        for c in range(W2_CHUNKS):
-            w2_codes = keep.tile([P, PASSES, CHUNK], U32, name="w2_codes_%d" % c, align_bytes=64)
-            w2_scales = keep.tile([P, PASSES, CHUNK], U8, name="w2_scales_%d" % c, align_bytes=64)
-            out_acc = [
-                psum.tile([P, CHUNK], F32, name="out_acc_%d" % i, tag="bank") for i in range(TILES)
-            ]
-            grouped = [regroup_weight_piece(nc, grouped_pool, w2_raw[(c, 0)])]
-            for g in range(PASSES):
-                if g + 1 < PASSES:
-                    grouped.append(regroup_weight_piece(nc, grouped_pool, w2_raw[(c, g + 1)]))
-                quantise(nc, grouped[g][:], w2_codes[:, g, :], w2_scales[:, g, :])
-                for i in range(TILES):
-                    tokens = slice(i * P, (i + 1) * P)
+        h_acc = {}
+        h_grouped = {}
+
+        def multiply_first(n):
+            m, i = divmod(n, TILES)
+            acc = psum.tile([P, PACK, P], F32, name="h_acc", tag="bank")
+            for t in range(PACK):
+                columns = slice(t * P, (t + 1) * P)
+                for g in range(PASSES):
                     nc.tensor.matmul_mx(
-                        out=out_acc[i][:],
-                        lhsT=h_codes[:, g, tokens].bitcast(FP8X4),
-                        lhsT_scale=h_scales[:, g, tokens],
-                        rhs=w2_codes[:, g, :].bitcast(FP8X4),
-                        rhs_scale=w2_scales[:, g, :],
+                        out=acc[:, t, :],
+                        lhsT=weight_codes[("w1", m)][:, g, columns].bitcast(FP8X4),
+                        lhsT_scale=weight_scales[("w1", m)][:, g, columns],
+                        rhs=sc_codes[:, i, g, :].bitcast(FP8X4),
+                        rhs_scale=sc_scales[:, i, g, :],
                         start=(g == 0),
                         stop=(g == PASSES - 1),
                     )
+            h_acc[n] = acc
+
+        def activate(n):
+            h = h_pool.tile([P, P, PACK], BF16, name="h_grouped", align_bytes=64)
+            nc.scalar.activation(
+                out=h[:],
+                in_=h_acc[n][:].rearrange("p t n -> p n t"),
+                func=ACT.Silu,
+                scale=inv_sqrt_ks,
+            )
+            h_grouped[n] = h
+
+        def quantise_h(n):
+            m, i = divmod(n, TILES)
+            tokens = slice(i * P, (i + 1) * P)
+            quantise(nc, h_grouped[n][:], h_codes[:, m, tokens], h_scales[:, m, tokens])
+
+        def multiply_second(c, g, i, out_acc):
+            tokens = slice(i * P, (i + 1) * P)
+            nc.tensor.matmul_mx(
+                out=out_acc[:],
+                lhsT=h_codes[:, g, tokens].bitcast(FP8X4),
+                lhsT_scale=h_scales[:, g, tokens],
+                rhs=weight_codes[("w2", c)][:, g, :].bitcast(FP8X4),
+                rhs_scale=weight_scales[("w2", c)][:, g, :],
+                start=(g == 0),
+                stop=(g == PASSES - 1),
+            )
+
+        out_by_tile = out.rearrange("(p i) n -> p i n", i=TILES)
+
+        def store(c, i, out_acc, on_vector):
+            result = store_pool.tile([P, CHUNK], F32, name="result")
+            if on_vector:
+                nc.vector.tensor_scalar_mul(out=result[:], in0=out_acc[:], scalar1=inv_sqrt_ks)
+            else:
+                nc.scalar.mul(out=result[:], in_=out_acc[:], mul=inv_sqrt_ks)
+            nc.sync.dma_start(
+                out=out_by_tile[:, i, c * CHUNK : (c + 1) * CHUNK], in_=result[:]
+            )
+
+        last_tile = TILES - 1
+        beside = {2: [0, 1], 3: [2], 4: [3], 5: [4]}
+        with tc.manual_schedule(
+            engines={mybir.EngineType.PE, mybir.EngineType.Activation, mybir.EngineType.DVE}
+        ):
+            for i in range(3):
+                flip_s(i)
+            for i in range(2):
+                group_s(i)
+            regroup(0)
+            quantise_s(0)
+            quantise_s(1)
+            quantise_piece(0)
             for i in range(TILES):
-                result = store_pool.tile([P, CHUNK], F32, name="result")
-                if c == W2_CHUNKS - 1 and i % 2 == 1:
-                    nc.vector.tensor_scalar_mul(
-                        out=result[:], in0=out_acc[i][:], scalar1=inv_sqrt_ks
-                    )
-                else:
-                    nc.scalar.mul(out=result[:], in_=out_acc[i][:], mul=inv_sqrt_ks)
-                nc.sync.dma_start(
-                    out=out_by_tile[:, i, c * CHUNK : (c + 1) * CHUNK], in_=result[:]
-                )
+                square_v(i)
+                if i + 2 < TILES:
+                    group_s(i + 2)
+                flip_v(i)
+                if i + 3 < TILES:
+                    flip_s(i + 3)
+                if i > 0:
+                    regroup(i)
+                    if i < last_tile:
+                        quantise_s(i + 1)
+                    group_v(i - 1)
+                    quantise_piece(i)
+                    quantise_v(i - 1)
+                for n in beside.get(i, []):
+                    multiply_first(n)
+                for n in beside.get(i - 1, []):
+                    activate(n)
+                for n in beside.get(i - 2, []):
+                    quantise_h(n)
+            group_v(last_tile)
+            quantise_v(last_tile)
+
+            piece = TILES
+            done = 5
+            to_activate = beside[5]
+            to_quantise = beside[4]
+            while to_activate or to_quantise:
+                regroup(piece)
+                if piece > TILES:
+                    quantise_piece(piece - 1)
+                piece += 1
+                new = list(range(done, min(done + 2, W1_CHUNKS * TILES)))
+                done += len(new)
+                for n in new:
+                    multiply_first(n)
+                for n in to_activate:
+                    activate(n)
+                for n in to_quantise:
+                    quantise_h(n)
+                to_quantise = to_activate
+                to_activate = new
+
+            for c in range(W2_CHUNKS):
+                while piece <= min(pieces.index(("w2", c, PASSES - 1)) + 1, len(pieces) - 1):
+                    regroup(piece)
+                    quantise_piece(piece - 1)
+                    piece += 1
+                last = c == W2_CHUNKS - 1
+                if last:
+                    quantise_piece(len(pieces) - 1)
+                accs = [
+                    psum.tile([P, CHUNK], F32, name="out_acc_%d" % i, tag="bank")
+                    for i in range(TILES)
+                ]
+                order = [(g, i) for g in range(PASSES) for i in range(TILES)]
+                if last:
+                    order = [(g, i) for i in range(TILES) for g in range(PASSES)]
+                for g, i in order:
+                    multiply_second(c, g, i, accs[i])
+                for i in range(TILES):
+                    store(c, i, accs[i], on_vector=last and i % 2 == 1)

@@ -260,11 +260,22 @@ def tile_selfinteraction_pa_kernel(tc, s, v, w1, w2, out):
                 out=out_by_tile[:, i, c * CHUNK : (c + 1) * CHUNK], in_=result[:]
             )
 
+        idle = keep.tile([P, CHUNK], BF16, name="idle")
+        nc.vector.memset(idle[:], 0.0)
+
+        def keep_busy(count):
+            unread = psum.tile([P, CHUNK], F32, name="unread", tag="bank")
+            for k in range(count):
+                nc.tensor.matmul(
+                    out=unread[:], lhsT=idle[:, 0:P], rhs=idle[:], start=True, stop=True
+                )
+
         last_tile = TILES - 1
         beside = {2: [0, 1], 3: [2], 4: [3], 5: [4]}
         with tc.manual_schedule(
             engines={mybir.EngineType.PE, mybir.EngineType.Activation, mybir.EngineType.DVE}
         ):
+            keep_busy(4)
             for i in range(3):
                 flip_s(i)
             for i in range(2):
@@ -280,6 +291,8 @@ def tile_selfinteraction_pa_kernel(tc, s, v, w1, w2, out):
                 flip_v(i)
                 if i + 3 < TILES:
                     flip_s(i + 3)
+                if i < last_tile:
+                    keep_busy(4 if i < 2 else 2 if i == 2 else 1)
                 if i > 0:
                     regroup(i)
                     if i < last_tile:

@@ -337,14 +337,13 @@ def tile_selfinteraction_pa_kernel(tc, s, v, w1, w2, out):
                 last = c == W2_CHUNKS - 1
                 if last:
                     quantise_piece(len(pieces) - 1)
-                accs = [
-                    psum.tile([P, CHUNK], F32, name="out_acc_%d" % i, tag="bank")
-                    for i in range(TILES)
-                ]
-                order = [(g, i) for g in range(PASSES) for i in range(TILES)]
-                if last:
-                    order = [(g, i) for i in range(TILES) for g in range(PASSES)]
-                for g, i in order:
-                    multiply_second(c, g, i, accs[i])
-                for i in range(TILES):
-                    store(c, i, accs[i], on_vector=last and i % 2 == 1)
+                for pair in range(TILES // 2):
+                    tiles = (2 * pair, 2 * pair + 1)
+                    accs = {}
+                    for i in tiles:
+                        accs[i] = psum.tile([P, CHUNK], F32, name="out_acc", tag="bank")
+                    for g in range(PASSES):
+                        for i in tiles:
+                            multiply_second(c, g, i, accs[i])
+                    for i in tiles:
+                        store(c, i, accs[i], on_vector=last and i % 2 == 1)

@@ -125,11 +125,13 @@ def tile_selfinteraction_pa_kernel(tc, s, v, w1, w2, out):
             s_flipped[i] = flipped
 
         def group_s(i):
-            flipped = s_flipped[i][:].rearrange("p t n -> p n t")
             both = small.tile([P, 2, P, PACK], BF16, name="s_grouped", align_bytes=64)
-            nc.scalar.copy(out=both[:, 0, :, :], in_=flipped)
-            nc.scalar.activation(out=both[:, 1, :, :], in_=flipped, func=ACT.Square)
+            nc.scalar.copy(out=both[:, 0, :, :], in_=s_flipped[i][:].rearrange("p t n -> p n t"))
             s_grouped[i] = both
+
+        def square_s(i):
+            both = s_grouped[i]
+            nc.vector.tensor_mul(out=both[:, 1, :, :], in0=both[:, 0, :, :], in1=both[:, 0, :, :])
 
         def quantise_s(i):
             quantise(
@@ -164,9 +166,13 @@ def tile_selfinteraction_pa_kernel(tc, s, v, w1, w2, out):
                     )
             vv0_flipped[i] = flipped
 
+        def on_scalar(i):
+            return i % 2 == 1
+
         def group_v(i):
             vv0 = small.tile([P, P, PACK], BF16, name="v_grouped", align_bytes=64)
-            nc.vector.tensor_copy(out=vv0[:], in_=vv0_flipped[i][:].rearrange("p t n -> p n t"))
+            copy = nc.scalar.copy if on_scalar(i) else nc.vector.tensor_copy
+            copy(out=vv0[:], in_=vv0_flipped[i][:].rearrange("p t n -> p n t"))
             v_grouped[i] = vv0
 
         def quantise_v(i):
@@ -236,29 +242,32 @@ def tile_selfinteraction_pa_kernel(tc, s, v, w1, w2, out):
             tokens = slice(i * P, (i + 1) * P)
             quantise(nc, h_grouped[n][:], h_codes[:, m, tokens], h_scales[:, m, tokens])
 
-        def multiply_second(c, g, i, out_acc):
+        whole = slice(0, CHUNK)
+
+        def multiply_second(c, g, i, out_acc, columns=whole):
             tokens = slice(i * P, (i + 1) * P)
             nc.tensor.matmul_mx(
-                out=out_acc[:],
+                out=out_acc[:, columns],
                 lhsT=h_codes[:, g, tokens].bitcast(FP8X4),
                 lhsT_scale=h_scales[:, g, tokens],
-                rhs=weight_codes[("w2", c)][:, g, :].bitcast(FP8X4),
-                rhs_scale=weight_scales[("w2", c)][:, g, :],
+                rhs=weight_codes[("w2", c)][:, g, columns].bitcast(FP8X4),
+                rhs_scale=weight_scales[("w2", c)][:, g, columns],
                 start=(g == 0),
                 stop=(g == PASSES - 1),
             )
 
         out_by_tile = out.rearrange("(p i) n -> p i n", i=TILES)
 
-        def store(c, i, out_acc, on_vector):
+        def store(c, i, out_acc, on_vector, columns=whole):
             result = store_pool.tile([P, CHUNK], F32, name="result")
             if on_vector:
-                nc.vector.tensor_scalar_mul(out=result[:], in0=out_acc[:], scalar1=inv_sqrt_ks)
+                nc.vector.tensor_scalar_mul(
+                    out=result[:, columns], in0=out_acc[:, columns], scalar1=inv_sqrt_ks
+                )
             else:
-                nc.scalar.mul(out=result[:], in_=out_acc[:], mul=inv_sqrt_ks)
-            nc.sync.dma_start(
-                out=out_by_tile[:, i, c * CHUNK : (c + 1) * CHUNK], in_=result[:]
-            )
+                nc.scalar.mul(out=result[:, columns], in_=out_acc[:, columns], mul=inv_sqrt_ks)
+            in_out = slice(c * CHUNK + columns.start, c * CHUNK + columns.stop)
+            nc.sync.dma_start(out=out_by_tile[:, i, in_out], in_=result[:, columns])
 
         idle = keep.tile([P, CHUNK], BF16, name="idle")
         nc.vector.memset(idle[:], 0.0)
@@ -271,7 +280,7 @@ def tile_selfinteraction_pa_kernel(tc, s, v, w1, w2, out):
                 )
 
         last_tile = TILES - 1
-        beside = {2: [0, 1], 3: [2], 4: [3], 5: [4]}
+        beside = {3: [0, 1], 4: [2], 5: [3]}
         with tc.manual_schedule(
             engines={mybir.EngineType.PE, mybir.EngineType.Activation, mybir.EngineType.DVE}
         ):
@@ -281,6 +290,8 @@ def tile_selfinteraction_pa_kernel(tc, s, v, w1, w2, out):
             for i in range(2):
                 group_s(i)
             regroup(0)
+            square_s(0)
+            square_s(1)
             quantise_s(0)
             quantise_s(1)
             quantise_piece(0)
@@ -288,17 +299,22 @@ def tile_selfinteraction_pa_kernel(tc, s, v, w1, w2, out):
                 square_v(i)
                 if i + 2 < TILES:
                     group_s(i + 2)
+                if i > 0 and on_scalar(i - 1):
+                    group_v(i - 1)
                 flip_v(i)
                 if i + 3 < TILES:
                     flip_s(i + 3)
                 if i < last_tile:
-                    keep_busy(4 if i < 2 else 2 if i == 2 else 1)
+                    keep_busy(4 if i < 3 else 1)
                 if i > 0:
                     regroup(i)
                     if i < last_tile:
-                        quantise_s(i + 1)
-                    group_v(i - 1)
+                        square_s(i + 1)
+                    if not on_scalar(i - 1):
+                        group_v(i - 1)
                     quantise_piece(i)
+                    if i < last_tile:
+                        quantise_s(i + 1)
                     quantise_v(i - 1)
                 for n in beside.get(i, []):
                     multiply_first(n)
@@ -310,7 +326,7 @@ def tile_selfinteraction_pa_kernel(tc, s, v, w1, w2, out):
             quantise_v(last_tile)
 
             piece = TILES
-            done = 5
+            done = 4
             to_activate = beside[5]
             to_quantise = beside[4]
             while to_activate or to_quantise:
@@ -339,6 +355,8 @@ def tile_selfinteraction_pa_kernel(tc, s, v, w1, w2, out):
                     quantise_piece(len(pieces) - 1)
                 for pair in range(TILES // 2):
                     tiles = (2 * pair, 2 * pair + 1)
+                    if last and last_tile in tiles:
+                        break
                     accs = {}
                     for i in tiles:
                         accs[i] = psum.tile([P, CHUNK], F32, name="out_acc", tag="bank")
@@ -347,3 +365,14 @@ def tile_selfinteraction_pa_kernel(tc, s, v, w1, w2, out):
                             multiply_second(c, g, i, accs[i])
                     for i in tiles:
                         store(c, i, accs[i], on_vector=last and i % 2 == 1)
+            c = W2_CHUNKS - 1
+            halves = (slice(0, CHUNK // 2), slice(CHUNK // 2, CHUNK))
+            for i, columns, on_vector in (
+                (last_tile - 1, whole, False),
+                (last_tile, halves[0], True),
+                (last_tile, halves[1], False),
+            ):
+                acc = psum.tile([P, CHUNK], F32, name="out_acc", tag="bank")
+                for g in range(PASSES):
+                    multiply_second(c, g, i, acc, columns)
+                store(c, i, acc, on_vector, columns)

@@ -24,7 +24,7 @@ CHUNK = 512
 W1_CHUNKS = KS // CHUNK
 W2_CHUNKS = G // CHUNK
 RAW_BUFS = 14
-SCALAR_PIECES = (8, 11, 14)
+SCALAR_PIECES = (8, 11, 14, 20)
 
 FLOPS = 2 * TOKENS * KS * (KS + G)
 
@@ -91,11 +91,13 @@ def tile_selfinteraction_pa_kernel(tc, s, v, w1, w2, out):
             raw[(name, chunk, g)] = load_weight_piece(nc, raw_pool, weights[name], chunk, g)
 
         load_s_pair(0)
-        for i in range(TILES):
-            load_piece(i)
+        load_piece(0)
+        load_v_tile(0)
+        for i in range(1, TILES):
+            if i < TILES // 2:
+                load_s_pair(i)
             load_v_tile(i)
-            if i < 2:
-                load_s_pair(i + 1)
+            load_piece(i)
         for n in range(TILES, len(pieces)):
             load_piece(n)
 
@@ -166,13 +168,9 @@ def tile_selfinteraction_pa_kernel(tc, s, v, w1, w2, out):
                     )
             vv0_flipped[i] = flipped
 
-        def on_scalar(i):
-            return i % 2 == 1
-
         def group_v(i):
             vv0 = small.tile([P, P, PACK], BF16, name="v_grouped", align_bytes=64)
-            copy = nc.scalar.copy if on_scalar(i) else nc.vector.tensor_copy
-            copy(out=vv0[:], in_=vv0_flipped[i][:].rearrange("p t n -> p n t"))
+            nc.scalar.copy(out=vv0[:], in_=vv0_flipped[i][:].rearrange("p t n -> p n t"))
             v_grouped[i] = vv0
 
         def quantise_v(i):
@@ -280,7 +278,7 @@ def tile_selfinteraction_pa_kernel(tc, s, v, w1, w2, out):
                 )
 
         last_tile = TILES - 1
-        beside = {3: [0, 1], 4: [2], 5: [3]}
+        beside = {3: [0, 1], 4: [2, 3], 5: [4]}
         with tc.manual_schedule(
             engines={mybir.EngineType.PE, mybir.EngineType.Activation, mybir.EngineType.DVE}
         ):
@@ -299,7 +297,7 @@ def tile_selfinteraction_pa_kernel(tc, s, v, w1, w2, out):
                 square_v(i)
                 if i + 2 < TILES:
                     group_s(i + 2)
-                if i > 0 and on_scalar(i - 1):
+                if i > 0:
                     group_v(i - 1)
                 flip_v(i)
                 if i + 3 < TILES:
@@ -310,8 +308,6 @@ def tile_selfinteraction_pa_kernel(tc, s, v, w1, w2, out):
                     regroup(i)
                     if i < last_tile:
                         square_s(i + 1)
-                    if not on_scalar(i - 1):
-                        group_v(i - 1)
                     quantise_piece(i)
                     if i < last_tile:
                         quantise_s(i + 1)
@@ -323,19 +319,21 @@ def tile_selfinteraction_pa_kernel(tc, s, v, w1, w2, out):
                 for n in beside.get(i - 2, []):
                     quantise_h(n)
             group_v(last_tile)
-            quantise_v(last_tile)
 
             piece = TILES
-            done = 4
+            waiting = list(range(TILES, W1_CHUNKS * TILES))
+            waiting.insert(3, last_tile)
             to_activate = beside[5]
             to_quantise = beside[4]
             while to_activate or to_quantise:
                 regroup(piece)
-                if piece > TILES:
+                if piece == TILES:
+                    quantise_v(last_tile)
+                else:
                     quantise_piece(piece - 1)
                 piece += 1
-                new = list(range(done, min(done + 2, W1_CHUNKS * TILES)))
-                done += len(new)
+                new = waiting[:2]
+                waiting = waiting[2:]
                 for n in new:
                     multiply_first(n)
                 for n in to_activate:
@@ -347,9 +345,13 @@ def tile_selfinteraction_pa_kernel(tc, s, v, w1, w2, out):
 
             for c in range(W2_CHUNKS):
                 while piece <= min(pieces.index(("w2", c, PASSES - 1)) + 1, len(pieces) - 1):
-                    regroup(piece)
+                    if piece not in grouped:
+                        regroup(piece)
                     quantise_piece(piece - 1)
                     piece += 1
+                for n in SCALAR_PIECES:
+                    if piece <= n <= piece + PASSES - 1:
+                        regroup(n)
                 last = c == W2_CHUNKS - 1
                 if last:
                     quantise_piece(len(pieces) - 1)

@@ -283,8 +283,11 @@ def tile_selfinteraction_pa_kernel(tc, s, v, w1, w2, out):
             engines={mybir.EngineType.PE, mybir.EngineType.Activation, mybir.EngineType.DVE}
         ):
             keep_busy(4)
-            for i in range(3):
-                flip_s(i)
+            flip_s(0)
+            flip_s(1)
+            keep_busy(4)
+            flip_s(2)
+            keep_busy(2)
             for i in range(2):
                 group_s(i)
             regroup(0)
@@ -303,7 +306,7 @@ def tile_selfinteraction_pa_kernel(tc, s, v, w1, w2, out):
                 if i + 3 < TILES:
                     flip_s(i + 3)
                 if i < last_tile:
-                    keep_busy(4 if i < 3 else 1)
+                    keep_busy(4 if i < 3 else 2)
                 if i > 0:
                     regroup(i)
                     if i < last_tile:

@@ -305,8 +305,8 @@ def tile_selfinteraction_pa_kernel(tc, s, v, w1, w2, out):
                 flip_v(i)
                 if i + 3 < TILES:
                     flip_s(i + 3)
-                if i < last_tile:
-                    keep_busy(4 if i < 3 else 2)
+                if i < 3:
+                    keep_busy(4)
                 if i > 0:
                     regroup(i)
                     if i < last_tile:

@@ -24,7 +24,7 @@ CHUNK = 512
 W1_CHUNKS = KS // CHUNK
 W2_CHUNKS = G // CHUNK
 RAW_BUFS = 14
-SCALAR_PIECES = (8, 11, 14, 20)
+SCALAR_PIECES = (8, 11, 14, 17)
 
 FLOPS = 2 * TOKENS * KS * (KS + G)
 
@@ -278,7 +278,8 @@ def tile_selfinteraction_pa_kernel(tc, s, v, w1, w2, out):
                 )
 
         last_tile = TILES - 1
-        beside = {3: [0, 1], 4: [2, 3], 5: [4]}
+        beside = {2: [0], 3: [1, 2], 4: [3]}
+        next_s = {1: 2, 2: 3, 3: 4, 5: 5}
         with tc.manual_schedule(
             engines={mybir.EngineType.PE, mybir.EngineType.Activation, mybir.EngineType.DVE}
         ):
@@ -306,28 +307,33 @@ def tile_selfinteraction_pa_kernel(tc, s, v, w1, w2, out):
                 if i + 3 < TILES:
                     flip_s(i + 3)
                 if i < 3:
-                    keep_busy(4)
+                    keep_busy(4 if i < 2 else 2)
                 if i > 0:
                     regroup(i)
-                    if i < last_tile:
-                        square_s(i + 1)
-                    quantise_piece(i)
-                    if i < last_tile:
-                        quantise_s(i + 1)
-                    quantise_v(i - 1)
+                    if i in next_s:
+                        square_s(next_s[i])
+                        quantise_piece(i)
+                        quantise_s(next_s[i])
+                        quantise_v(i - 1)
+                    else:
+                        quantise_v(i - 1)
+                        quantise_piece(i)
                 for n in beside.get(i, []):
                     multiply_first(n)
-                for n in beside.get(i - 1, []):
-                    activate(n)
                 for n in beside.get(i - 2, []):
+                    activate(n)
+                for n in beside.get(i - 3, []):
                     quantise_h(n)
+            for n in beside[4]:
+                activate(n)
             group_v(last_tile)
 
             piece = TILES
             waiting = list(range(TILES, W1_CHUNKS * TILES))
-            waiting.insert(3, last_tile)
-            to_activate = beside[5]
-            to_quantise = beside[4]
+            waiting.insert(4, last_tile - 1)
+            waiting.insert(6, last_tile)
+            to_activate = []
+            to_quantise = beside[3] + beside[4]
             while to_activate or to_quantise:
                 regroup(piece)
                 if piece == TILES:
@@ -352,10 +358,10 @@ def tile_selfinteraction_pa_kernel(tc, s, v, w1, w2, out):
                         regroup(piece)
                     quantise_piece(piece - 1)
                     piece += 1
-                for n in SCALAR_PIECES:
-                    if piece <= n <= piece + PASSES - 1:
-                        regroup(n)
                 last = c == W2_CHUNKS - 1
+                last_of_next = pieces.index(("w2", c, PASSES - 1)) + PASSES
+                if last_of_next in SCALAR_PIECES and last_of_next not in grouped:
+                    regroup(last_of_next)
                 if last:
                     quantise_piece(len(pieces) - 1)
                 for pair in range(TILES // 2):

import math
from contextlib import ExitStack

import concourse.mybir as mybir
from concourse.masks import make_identity

BF16 = mybir.dt.bfloat16
F32 = mybir.dt.float32
U32 = mybir.dt.uint32
U8 = mybir.dt.uint8
FP8X4 = mybir.dt.float8_e4m3fn_x4
ACT = mybir.ActivationFunctionType

P = 128
PACK = 4
K_PASS = P * PACK
TOKENS = 768
TILES = TOKENS // P
C = 512
KS = 3 * C
PASSES = KS // K_PASS
G = 5 * C
CHUNK = 512
W1_CHUNKS = KS // CHUNK
W2_CHUNKS = G // CHUNK
RAW_BUFS = 14
SCALAR_PIECES = (8, 11, 14, 17)

FLOPS = 2 * TOKENS * KS * (KS + G)


def load_weight_piece(nc, raw_pool, w, chunk, g):
    by_pass = w.rearrange("(g t p) n -> g p t n", t=PACK, p=P)
    raw = raw_pool.tile([P, PACK, CHUNK], BF16, name="raw")
    nc.sync.dma_start(out=raw[:], in_=by_pass[g, :, :, chunk * CHUNK : (chunk + 1) * CHUNK])
    return raw


def regroup_weight_piece(nc, grouped_pool, raw, on_scalar):
    grouped = grouped_pool.tile([P, CHUNK, PACK], BF16, name="grouped", align_bytes=64)
    copy = nc.scalar.copy if on_scalar else nc.vector.tensor_copy
    copy(
        out=grouped[:].rearrange("p (c i) t -> p c t i", i=4),
        in_=raw[:].rearrange("p t (c i) -> p c t i", i=4),
    )
    return grouped


def quantise(nc, grouped, codes, scales):
    nc.vector.quantize_mx(
        out=codes.bitcast(FP8X4), scales=scales, in_=grouped.rearrange("p c t -> p (c t)")
    )


def tile_selfinteraction_pa_kernel(tc, s, v, w1, w2, out):
    nc = tc.nc
    inv_sqrt_ks = 1.0 / math.sqrt(KS)

    with ExitStack() as ctx:
        keep = ctx.enter_context(tc.tile_pool(name="keep", bufs=1))
        raw_pool = ctx.enter_context(tc.tile_pool(name="raw_pool", bufs=RAW_BUFS))
        grouped_pool = ctx.enter_context(tc.tile_pool(name="grouped_pool", bufs=4))
        work = ctx.enter_context(tc.tile_pool(name="work", bufs=3))
        small = ctx.enter_context(tc.tile_pool(name="small", bufs=4))
        h_pool = ctx.enter_context(tc.tile_pool(name="h_pool", bufs=8))
        store_pool = ctx.enter_context(tc.tile_pool(name="store_pool", bufs=TILES))
        psum = ctx.enter_context(tc.psum_pool(name="psum", bufs=8))

        s_by_pair = s.rearrange("(p i) c -> p i c", i=TILES)
        v_by_tile = v.rearrange("(p i) c d -> p i (c d)", i=TILES)
        s_sb = []
        v_sb = []
        raw = {}

        def load_s_pair(j):
            s_j = keep.tile([P, 2, C], BF16, name="s_%d" % j)
            nc.sync.dma_start(out=s_j[:], in_=s_by_pair[:, 2 * j : 2 * j + 2, :])
            s_sb.append(s_j)

        def load_v_tile(i):
            v_i = keep.tile([P, 3 * C], BF16, name="v_%d" % i)
            nc.sync.dma_start(out=v_i[:], in_=v_by_tile[:, i, :])
            v_sb.append(v_i)

        pieces = [("w1", m, g) for m in range(W1_CHUNKS) for g in range(PASSES)]
        pieces += [("w2", c, g) for c in range(W2_CHUNKS) for g in range(PASSES)]
        weights = {"w1": w1, "w2": w2}

        def load_piece(n):
            name, chunk, g = pieces[n]
            raw[(name, chunk, g)] = load_weight_piece(nc, raw_pool, weights[name], chunk, g)

        load_s_pair(0)
        load_piece(0)
        load_v_tile(0)
        for i in range(1, TILES):
            if i < TILES // 2:
                load_s_pair(i)
            load_v_tile(i)
            load_piece(i)
        for n in range(TILES, len(pieces)):
            load_piece(n)

        ident = keep.tile([P, P], BF16, name="ident")
        make_identity(nc, ident[:])
        ident_f32 = keep.tile([P, P], F32, name="ident_f32")
        make_identity(nc, ident_f32[:])

        warm = keep.tile([P, 1], F32, name="warm")
        nc.vector.memset(warm[:], 0.0)
        nc.scalar.activation(out=warm[:], in_=warm[:], func=ACT.Silu)

        sc_codes = keep.tile([P, TILES, PASSES, P], U32, name="sc_codes", align_bytes=64)
        sc_scales = keep.tile([P, TILES, PASSES, P], U8, name="sc_scales", align_bytes=64)

        s_flipped = {}
        s_grouped = {}
        v_squares = {}
        vv0_flipped = {}
        v_grouped = {}

        def flip_s(i):
            s_i = s_sb[i // 2][:, i % 2, :]
            flipped = psum.tile([P, PACK, P], BF16, name="s_flipped", tag="bank")
            for t in range(PACK):
                nc.tensor.transpose(flipped[:, t, :], s_i[:, t * P : (t + 1) * P], ident[:])
            s_flipped[i] = flipped

        def group_s(i):
            both = small.tile([P, 2, P, PACK], BF16, name="s_grouped", align_bytes=64)
            nc.scalar.copy(out=both[:, 0, :, :], in_=s_flipped[i][:].rearrange("p t n -> p n t"))
            s_grouped[i] = both

        def square_s(i):
            both = s_grouped[i]
            nc.vector.tensor_mul(out=both[:, 1, :, :], in0=both[:, 0, :, :], in1=both[:, 0, :, :])

        def quantise_s(i):
            quantise(
                nc,
                s_grouped[i][:].rearrange("p g n t -> p (g n) t"),
                sc_codes[:, i, 0:2, :].rearrange("p g n -> p (g n)"),
                sc_scales[:, i, 0:2, :].rearrange("p g n -> p (g n)"),
            )

        def square_v(i):
            squares = work.tile([P, 3, C], F32, name="squares")
            nc.scalar.activation(
                out=squares[:],
                in_=v_sb[i][:].rearrange("p (c d) -> p d c", d=3),
                func=ACT.Square,
                scale=3.0**-0.25,
            )
            v_squares[i] = squares

        def flip_v(i):
            squares = v_squares[i]
            flipped = psum.tile([P, PACK, P], F32, name="vv0_flipped", tag="bank")
            for t in range(PACK):
                for d in range(3):
                    nc.tensor.matmul(
                        out=flipped[:, t, :],
                        lhsT=squares[:, d, t * P : (t + 1) * P],
                        rhs=ident_f32[:],
                        is_transpose=True,
                        start=(d == 0),
                        stop=(d == 2),
                    )
            vv0_flipped[i] = flipped

        def group_v(i):
            vv0 = small.tile([P, P, PACK], BF16, name="v_grouped", align_bytes=64)
            nc.scalar.copy(out=vv0[:], in_=vv0_flipped[i][:].rearrange("p t n -> p n t"))
            v_grouped[i] = vv0

        def quantise_v(i):
            quantise(nc, v_grouped[i][:], sc_codes[:, i, 2, :], sc_scales[:, i, 2, :])

        weight_codes = {}
        weight_scales = {}
        for name, chunks in (("w1", W1_CHUNKS), ("w2", W2_CHUNKS)):
            for c in range(chunks):
                weight_codes[(name, c)] = keep.tile(
                    [P, PASSES, CHUNK], U32, name="%s_codes_%d" % (name, c), align_bytes=64
                )
                weight_scales[(name, c)] = keep.tile(
                    [P, PASSES, CHUNK], U8, name="%s_scales_%d" % (name, c), align_bytes=64
                )
        grouped = {}

        def regroup(n):
            grouped[n] = regroup_weight_piece(
                nc, grouped_pool, raw[pieces[n]], on_scalar=n in SCALAR_PIECES
            )

        def quantise_piece(n):
            name, chunk, g = pieces[n]
            quantise(
                nc,
                grouped[n][:],
                weight_codes[(name, chunk)][:, g, :],
                weight_scales[(name, chunk)][:, g, :],
            )

        h_codes = keep.tile([P, PASSES, TOKENS], U32, name="h_codes", align_bytes=64)
        h_scales = keep.tile([P, PASSES, TOKENS], U8, name="h_scales", align_bytes=64)

        h_acc = {}
        h_grouped = {}

        def multiply_first(n):
            m, i = divmod(n, TILES)
            acc = psum.tile([P, PACK, P], F32, name="h_acc", tag="bank")
            for t in range(PACK):
                columns = slice(t * P, (t + 1) * P)
                for g in range(PASSES):
                    nc.tensor.matmul_mx(
                        out=acc[:, t, :],
                        lhsT=weight_codes[("w1", m)][:, g, columns].bitcast(FP8X4),
                        lhsT_scale=weight_scales[("w1", m)][:, g, columns],
                        rhs=sc_codes[:, i, g, :].bitcast(FP8X4),
                        rhs_scale=sc_scales[:, i, g, :],
                        start=(g == 0),
                        stop=(g == PASSES - 1),
                    )
            h_acc[n] = acc

        def activate(n):
            h = h_pool.tile([P, P, PACK], BF16, name="h_grouped", align_bytes=64)
            nc.scalar.activation(
                out=h[:],
                in_=h_acc[n][:].rearrange("p t n -> p n t"),
                func=ACT.Silu,
                scale=inv_sqrt_ks,
            )
            h_grouped[n] = h

        def quantise_h(n):
            m, i = divmod(n, TILES)
            tokens = slice(i * P, (i + 1) * P)
            quantise(nc, h_grouped[n][:], h_codes[:, m, tokens], h_scales[:, m, tokens])

        whole = slice(0, CHUNK)

        def multiply_second(c, g, i, out_acc, columns=whole):
            tokens = slice(i * P, (i + 1) * P)
            nc.tensor.matmul_mx(
                out=out_acc[:, columns],
                lhsT=h_codes[:, g, tokens].bitcast(FP8X4),
                lhsT_scale=h_scales[:, g, tokens],
                rhs=weight_codes[("w2", c)][:, g, columns].bitcast(FP8X4),
                rhs_scale=weight_scales[("w2", c)][:, g, columns],
                start=(g == 0),
                stop=(g == PASSES - 1),
            )

        out_by_tile = out.rearrange("(p i) n -> p i n", i=TILES)

        def store(c, i, out_acc, on_vector, columns=whole):
            result = store_pool.tile([P, CHUNK], F32, name="result")
            if on_vector:
                nc.vector.tensor_scalar_mul(
                    out=result[:, columns], in0=out_acc[:, columns], scalar1=inv_sqrt_ks
                )
            else:
                nc.scalar.mul(out=result[:, columns], in_=out_acc[:, columns], mul=inv_sqrt_ks)
            in_out = slice(c * CHUNK + columns.start, c * CHUNK + columns.stop)
            nc.sync.dma_start(out=out_by_tile[:, i, in_out], in_=result[:, columns])

        idle = keep.tile([P, CHUNK], BF16, name="idle")
        nc.vector.memset(idle[:], 0.0)

        def keep_busy(count):
            unread = psum.tile([P, CHUNK], F32, name="unread", tag="bank")
            for k in range(count):
                nc.tensor.matmul(
                    out=unread[:], lhsT=idle[:, 0:P], rhs=idle[:], start=True, stop=True
                )

        last_tile = TILES - 1
        beside = {2: [0], 3: [1, 2], 4: [3]}
        next_s = {1: 2, 2: 3, 3: 4, 5: 5}
        with tc.manual_schedule(
            engines={mybir.EngineType.PE, mybir.EngineType.Activation, mybir.EngineType.DVE}
        ):
            keep_busy(4)
            flip_s(0)
            flip_s(1)
            keep_busy(4)
            flip_s(2)
            keep_busy(2)
            for i in range(2):
                group_s(i)
            regroup(0)
            square_s(0)
            square_s(1)
            quantise_s(0)
            quantise_s(1)
            quantise_piece(0)
            for i in range(TILES):
                square_v(i)
                if i + 2 < TILES:
                    group_s(i + 2)
                if i > 0:
                    group_v(i - 1)
                flip_v(i)
                if i + 3 < TILES:
                    flip_s(i + 3)
                if i < 3:
                    keep_busy(4 if i < 2 else 2)
                if i > 0:
                    regroup(i)
                    if i in next_s:
                        square_s(next_s[i])
                        quantise_piece(i)
                        quantise_s(next_s[i])
                        quantise_v(i - 1)
                    else:
                        quantise_v(i - 1)
                        quantise_piece(i)
                for n in beside.get(i, []):
                    multiply_first(n)
                for n in beside.get(i - 2, []):
                    activate(n)
                for n in beside.get(i - 3, []):
                    quantise_h(n)
            for n in beside[4]:
                activate(n)
            group_v(last_tile)

            piece = TILES
            waiting = list(range(TILES, W1_CHUNKS * TILES))
            waiting.insert(4, last_tile - 1)
            waiting.insert(6, last_tile)
            to_activate = []
            to_quantise = beside[3] + beside[4]
            while to_activate or to_quantise:
                regroup(piece)
                if piece == TILES:
                    quantise_v(last_tile)
                else:
                    quantise_piece(piece - 1)
                piece += 1
                new = waiting[:2]
                waiting = waiting[2:]
                for n in new:
                    multiply_first(n)
                for n in to_activate:
                    activate(n)
                for n in to_quantise:
                    quantise_h(n)
                to_quantise = to_activate
                to_activate = new

            for c in range(W2_CHUNKS):
                while piece <= min(pieces.index(("w2", c, PASSES - 1)) + 1, len(pieces) - 1):
                    if piece not in grouped:
                        regroup(piece)
                    quantise_piece(piece - 1)
                    piece += 1
                last = c == W2_CHUNKS - 1
                last_of_next = pieces.index(("w2", c, PASSES - 1)) + PASSES
                if last_of_next in SCALAR_PIECES and last_of_next not in grouped:
                    regroup(last_of_next)
                if last:
                    quantise_piece(len(pieces) - 1)
                for pair in range(TILES // 2):
                    tiles = (2 * pair, 2 * pair + 1)
                    if last and last_tile in tiles:
                        break
                    accs = {}
                    for i in tiles:
                        accs[i] = psum.tile([P, CHUNK], F32, name="out_acc", tag="bank")
                    for g in range(PASSES):
                        for i in tiles:
                            multiply_second(c, g, i, accs[i])
                    for i in tiles:
                        store(c, i, accs[i], on_vector=last and i % 2 == 1)
            c = W2_CHUNKS - 1
            halves = (slice(0, CHUNK // 2), slice(CHUNK // 2, CHUNK))
            for i, columns, on_vector in (
                (last_tile - 1, whole, False),
                (last_tile, halves[0], True),
                (last_tile, halves[1], False),
            ):
                acc = psum.tile([P, CHUNK], F32, name="out_acc", tag="bank")
                for g in range(PASSES):
                    multiply_second(c, g, i, acc, columns)
                store(c, i, acc, on_vector, columns)
